import numpy as np
import ml_dtypes


def mxq(x, axis, fmt="e4m3"):
    dtype, down = {"e4m3": (ml_dtypes.float8_e4m3fn, 7), "e5m2": (ml_dtypes.float8_e5m2, 14)}[fmt]
    v = np.moveaxis(np.asarray(x, np.float32).astype(ml_dtypes.bfloat16).astype(np.float64), axis, -1)
    blocks = v.reshape(v.shape[:-1] + (-1, 32))
    amax = np.abs(blocks).max(-1, keepdims=True)
    byte = np.maximum(np.where(amax > 0, np.frexp(amax)[1] - 1 + 127, 0) - down, 1)
    scale = np.exp2(byte - 127.0)
    codes = (blocks / scale).astype(np.float32).astype(dtype).astype(np.float64)
    return np.moveaxis((codes * scale).reshape(v.shape), -1, axis)


WIDE = False


def mx_kscale(k):
    if not WIDE:
        return np.ones(k)
    levels = np.array([18, -18])
    if k % 512:
        return np.exp2(np.random.permutation(np.resize(levels, k // 32))).repeat(32)
    a = np.empty((k // 512, 16))
    for p in range(k // 512):
        a[p, :8] = np.random.permutation(np.resize(levels, 8))
        for g in range(8):
            far = levels[np.abs(levels - a[p, g]) >= 10]
            a[p, g + 8] = far[np.random.randint(len(far))]
    return np.exp2(a.ravel()).repeat(32)


BF16 = ml_dtypes.bfloat16


def bf(x):
    return np.asarray(x, np.float32).astype(BF16)


def f64(x):
    return np.asarray(x).astype(np.float64)


B, S, H, HO, E = 4, 256, 512, 1024, 4
T = B * S


def softmax_last(l):
    ex = np.exp(l - l.max(-1, keepdims=True))
    return ex / ex.sum(-1, keepdims=True)


def setup_inputs():
    s = mx_kscale(T).reshape(B, S, 1)
    u = mx_kscale(HO)
    h0 = bf(np.random.standard_normal((B, S, H)))
    op_logits = bf(np.random.standard_normal((B, S, E)) * 1.3)
    We0 = bf(np.random.standard_normal((E, H, HO)) / np.sqrt(H))
    be = bf(np.random.standard_normal((E, HO)) * 0.3)
    g0 = bf(np.random.standard_normal((B, S, HO)) * np.exp2(np.random.randint(-6, 1, (B, S, 1))) * 4.0)
    op_w = softmax_last(f64(op_logits))
    return {"hidden_states": bf(f64(h0) * s),
            "op_logits": op_logits,
            "We": bf(f64(We0) / u),
            "be": be,
            "op_w": np.asarray(op_w, np.float32),
            "grad_out": bf(f64(g0) / s * u)}


def reference(hidden_states, op_logits, We, be, op_w, grad_out):
    h = f64(hidden_states).reshape(T, H)
    p = f64(op_w).reshape(T, E)
    g = f64(grad_out).reshape(T, HO)
    dz = (p[:, :, None] * g[:, None, :]).reshape(T, E * HO)
    wt = f64(We).transpose(1, 0, 2).reshape(H, E * HO)
    dh = mxq(dz, 1, "e5m2") @ mxq(wt, 1, "e4m3").T
    dw = mxq(h, 0, "e4m3").T @ mxq(dz, 0, "e5m2")
    return dh.reshape(B, S, H), dw.reshape(H, E, HO).transpose(1, 0, 2)

from contextlib import ExitStack

import concourse.mybir as mybir
from concourse.masks import make_identity

F32 = mybir.dt.float32
BF16 = mybir.dt.bfloat16
U32 = mybir.dt.uint32
U8 = mybir.dt.uint8
E4M3 = mybir.dt.float8_e4m3fn_x4
E5M2 = mybir.dt.float8_e5m2_x4
MULT = mybir.AluOpType.mult

P = 128
E, H, HO, T = 4, 512, 1024, 1024
FLOPS = 2 * 2 * T * H * E * HO
BYTES = 2 * (T * H + E * H * HO + T * HO) + 4 * T * E + 4 * (T * H + E * H * HO)

F_ORDER = [(0, 0), (1, 0), (2, 0), (3, 0), (0, 1), (1, 1), (2, 1), (3, 1)]
T_ORDER = [(0, 0), (1, 0), (0, 1), (1, 1), (2, 0), (2, 1), (3, 0), (3, 1)]


def tile_enhancedmathematicalreasoning_pa_v_kernel(
    tc, hidden_states, op_logits, We, be, op_w, grad_out, out_0, out_1
):
    nc = tc.nc
    h_view = hidden_states.flatten_outer_dims().rearrange("(g p j) w -> g p j w", g=2, j=4)
    g_view = grad_out.flatten_outer_dims().rearrange("(g p j) w -> g p j w", g=2, j=4)
    w_view = We.rearrange("e (a p) w -> e p a w", p=P)
    p_view = op_w.flatten_outer_dims().rearrange("(g p j) e -> p g (j e)", g=2, j=4)
    o0_view = out_0.flatten_outer_dims().rearrange("(g p j) w -> g j p w", g=2, j=4)
    o1_view = out_1.rearrange("e (m p) w -> e m p w", p=P)

    with ExitStack() as ctx:
        keep = ctx.enter_context(tc.tile_pool(name="keep", bufs=1))
        wraw_pool = ctx.enter_context(tc.tile_pool(name="wraw", bufs=3))
        nat_pool = ctx.enter_context(tc.tile_pool(name="nat", bufs=5))
        int_pool = ctx.enter_context(tc.tile_pool(name="int", bufs=4))
        gf_pool = ctx.enter_context(tc.tile_pool(name="gf", bufs=6))
        gw_pool = ctx.enter_context(tc.tile_pool(name="gw", bufs=3))
        ct_pool = ctx.enter_context(tc.tile_pool(name="ct", bufs=12))
        cf_pool = ctx.enter_context(tc.tile_pool(name="cf", bufs=4))
        st_pool = ctx.enter_context(tc.tile_pool(name="st", bufs=5))
        s0_pool = ctx.enter_context(tc.tile_pool(name="s0", bufs=4))
        acc_pool = ctx.enter_context(tc.psum_pool(name="acc", bufs=1))
        rot_pool = ctx.enter_context(tc.psum_pool(name="rot", bufs=4))

        ident = keep.tile([P, P], F32, name="ident")
        make_identity(nc, ident[:])
        warm = keep.tile([P, 2], F32, name="warm")
        nc.gpsimd.memset(warm[:], 0.0)
        nc.scalar.copy(out=warm[:, 1:2], in_=warm[:, 0:1])

        p_sb = keep.tile([P, 2, 16], F32, name="p_sb")
        g_sb = [keep.tile([P, 4, HO], BF16, name=f"g_sb{g}") for g in range(2)]
        h_sb = [keep.tile([P, 4, H], BF16, name=f"h_sb{g}") for g in range(2)]
        w_raw = {}
        nc.sync.dma_start(out=p_sb[:], in_=p_view)
        for j in range(4):
            nc.sync.dma_start(out=g_sb[0][:, j, :], in_=g_view[0, :, j, :])

        def load_w(e):
            raw = wraw_pool.tile([P, 4, HO], BF16, name="w_raw", tag="w_raw")
            for a in (0, 2):
                nc.sync.dma_start(out=raw[:, a : a + 2, :], in_=w_view[e, :, a : a + 2, :])
            w_raw[e] = raw

        load_w(0)
        load_w(1)
        load_w(2)
        nc.sync.dma_start(out=h_sb[0][:], in_=h_view[0])
        nc.sync.dma_start(out=g_sb[1][:], in_=g_view[1])
        nc.sync.dma_start(out=h_sb[1][:], in_=h_view[1])
        load_w(3)

        nat = {}
        gf = {}
        cf = {}
        gw = {}
        cw = {}
        ti = {}
        ct = {}
        gh = {}
        ch = {}
        acc = {}

        def ts(cell):
            e, g = cell
            tile = nat_pool.tile([P, 4, HO], BF16, name="nat", tag="nat", align_bytes=64)
            nat[cell] = tile
            for j in range(4):
                nc.vector.tensor_scalar(
                    out=tile[:, j, :].rearrange("p (u w x) -> p u w x", u=2, x=2),
                    in0=g_sb[g][:, j, :].rearrange("p (w u x) -> p u w x", u=2, x=2),
                    scalar1=p_sb[:, g, 4 * j + e : 4 * j + e + 1],
                    scalar2=None,
                    op0=MULT,
                )

        def evac(bank, dst):
            nc.scalar.copy(
                out=dst.rearrange("p (s r u) -> p s r u", s=2, u=2),
                in_=bank[:].rearrange("p (s u r) -> p s r u", s=2, u=2),
            )

        def tr(cell):
            words = nat[cell][:].rearrange("p j w -> p (j w)").bitcast(F32)
            for c in range(2):
                dst = gf_pool.tile([P, 2048], BF16, name="gf", tag="gf", align_bytes=64)
                gf[cell, c] = dst
                for jp in range(2):
                    bank = rot_pool.tile([P, 512], F32, name="rot", tag="rot")
                    for s in range(2):
                        for u in range(2):
                            w0 = (2 * jp + s) * 512 + u * 256 + c * 128
                            k = (2 * s + u) * 128
                            nc.tensor.transpose(bank[:, k : k + 128], words[:, w0 : w0 + 128], ident[:])
                    evac(bank, dst[:].bitcast(F32)[:, jp * 512 : (jp + 1) * 512])

        def trw(e):
            words = w_raw[e][:].rearrange("p a w -> p (a w)").bitcast(F32)
            for c in range(2):
                dst = gw_pool.tile([P, 2048], BF16, name="gw", tag="gw", align_bytes=64)
                gw[e, c] = dst
                for ap in range(2):
                    bank = rot_pool.tile([P, 512], F32, name="rot", tag="rot")
                    for s in range(2):
                        for u in range(2):
                            w0 = (2 * ap + s) * 512 + c * 256 + u
                            k = (2 * s + u) * 128
                            nc.tensor.transpose(bank[:, k : k + 128], words[:, w0 : w0 + 255 : 2], ident[:])
                    evac(bank, dst[:].bitcast(F32)[:, ap * 512 : (ap + 1) * 512])

        def quant(pool, tag, src, fmt):
            codes = pool.tile([P, 512], U32, name="c_" + tag, tag="c_" + tag, align_bytes=64)
            scales = pool.tile([P, 512], U8, name="s_" + tag, tag="s_" + tag, align_bytes=64)
            nc.vector.quantize_mx(out=codes[:].bitcast(fmt), scales=scales[:], in_=src)
            return codes, scales

        def qf(cell, c):
            cf[cell, c] = quant(cf_pool, "cf", gf[cell, c][:], E5M2)

        def qw(e, c):
            cw[e, c] = quant(keep, f"cw{e}{c}", gw[e, c][:], E4M3)

        def int_h(g):
            tile = gw_pool.tile([P, 2048], BF16, name="gw", tag="gw", align_bytes=64)
            gh[g] = tile
            nc.scalar.copy(
                out=tile[:].rearrange("p (w j) -> p w j", j=4),
                in_=h_sb[g][:].rearrange("p j w -> p w j"),
            )

        def qh(g):
            ch[g] = quant(keep, f"ch{g}", gh[g][:], E4M3)

        def int_t(cell, c):
            tile = int_pool.tile([P, 2048], BF16, name="ti", tag="ti", align_bytes=64)
            ti[cell, c] = tile
            nc.vector.tensor_copy(
                out=tile[:].rearrange("p (u w j) -> p u w j", u=2, j=4),
                in_=nat[cell][:].rearrange("p j (u c w) -> p c u w j", u=2, c=2)[:, c],
            )

        def qt(cell, c):
            ct[cell, c] = quant(ct_pool, "ct", ti[cell, c][:], E5M2)

        def mx(out, lhs, l0, lfmt, rhs, rfmt, start, stop):
            nc.tensor.matmul_mx(
                out=out,
                lhsT=lhs[0][:, l0 : l0 + 128].bitcast(lfmt),
                lhsT_scale=lhs[1][:, l0 : l0 + 128],
                rhs=rhs[0][:].bitcast(rfmt),
                rhs_scale=rhs[1][:],
                start=start,
                stop=stop,
            )

        def mm0(cell):
            e, g = cell
            if e == 0:
                for j in range(4):
                    acc[g, j] = acc_pool.tile([P, 512], F32, name=f"acc{j}", tag=f"acc{j}")
            for c in range(2):
                for j in range(4):
                    mx(acc[g, j][:], cf[cell, c], 128 * j, E5M2, cw[e, c], E4M3,
                       e == 0 and c == 0, e == 3 and c == 1)
            if e == 3:
                for j in range(4):
                    stage = s0_pool.tile([P, 512], F32, name="s0", tag="s0")
                    nc.scalar.copy(out=stage[:], in_=acc[g, j][:])
                    nc.sync.dma_start(out=o0_view[g, j], in_=stage[:])

        def ev1(eng, bank, dst):
            args = dict(
                out=dst.rearrange("p (w u x) -> p w u x", u=2, x=2),
                in_=bank[:].rearrange("p (u w x) -> p w u x", u=2, x=2),
            )
            if eng == 0:
                nc.scalar.copy(**args)
            else:
                nc.vector.tensor_copy(**args)

        def mm1(e, ms):
            for m in ms:
                stage = st_pool.tile([P, HO], F32, name="st", tag="st")
                for c in range(2):
                    bank = rot_pool.tile([P, 512], F32, name="rot", tag="rot")
                    for g in range(2):
                        mx(bank[:], ch[g], 128 * m, E4M3, ct[(e, g), c], E5M2, g == 0, g == 1)
                    ev1(0, bank, stage[:, 512 * c : 512 * c + 512])
                nc.sync.dma_start(out=o1_view[e, m], in_=stage[:])

        with tc.manual_schedule():
            ts(F_ORDER[0])
            tr(F_ORDER[0])
            trw(0)
            ts(F_ORDER[1])
            ts(F_ORDER[2])
            tr(F_ORDER[1])
            trw(1)
            banks = {}
            for i in range(8):
                if i + 2 < 8:
                    tr(F_ORDER[i + 2])
                if i + 2 < 4:
                    trw(i + 2)
                if i < 2:
                    int_h(i)
                int_t(T_ORDER[i], 0)
                int_t(T_ORDER[i], 1)
                qf(F_ORDER[i], 0)
                qt(T_ORDER[i], 0)
                qf(F_ORDER[i], 1)
                qt(T_ORDER[i], 1)
                if i < 4:
                    qw(i, 0)
                    qw(i, 1)
                if i in (1, 2):
                    qh(i - 1)
                if i + 3 < 8:
                    ts(F_ORDER[i + 3])
                if i == 3:
                    mm1(0, range(4))
                if i == 4:
                    mm1(1, range(2))
                if i == 5:
                    mm1(1, range(2, 4))
                if i == 6:
                    mm1(2, range(4))
                mm0(F_ORDER[i])
            stages = [st_pool.tile([P, HO], F32, name="st", tag="st") for m in range(4)]
            for c in range(2):
                for m in range(4):
                    if c == 0:
                        banks[m, c] = rot_pool.tile([P, 512], F32, name="rot", tag="rot")
                    else:
                        banks[m, c] = acc_pool.tile([P, 512], F32, name=f"acc{m}", tag=f"acc{m}")
                    mx(banks[m, c][:], ch[0], 128 * m, E4M3, ct[(3, 0), c], E5M2, True, False)
            for c in range(2):
                for m in range(4):
                    mx(banks[m, c][:], ch[1], 128 * m, E4M3, ct[(3, 1), c], E5M2, False, True)
                    ev1(m % 2, banks[m, c], stages[m][:, 512 * c : 512 * c + 512])
                    nc.sync.dma_start(
                        out=o1_view[3, m][:, 512 * c : 512 * c + 512],
                        in_=stages[m][:, 512 * c : 512 * c + 512],
                    )
